import numpy as np
import ml_dtypes


def mxq(x, axis, fmt="e4m3"):
    dtype, down = {"e4m3": (ml_dtypes.float8_e4m3fn, 7), "e5m2": (ml_dtypes.float8_e5m2, 14)}[fmt]
    v = np.moveaxis(np.asarray(x, np.float32).astype(ml_dtypes.bfloat16).astype(np.float64), axis, -1)
    blocks = v.reshape(v.shape[:-1] + (-1, 32))
    amax = np.abs(blocks).max(-1, keepdims=True)
    byte = np.maximum(np.where(amax > 0, np.frexp(amax)[1] - 1 + 127, 0) - down, 1)
    scale = np.exp2(byte - 127.0)
    codes = (blocks / scale).astype(np.float32).astype(dtype).astype(np.float64)
    return np.moveaxis((codes * scale).reshape(v.shape), -1, axis)


WIDE = False


def mx_kscale(k):
    if not WIDE:
        return np.ones(k)
    levels = np.array([10, -10, 5, -5, 0])
    a = np.random.permutation(np.resize(levels, k // 512 * 4)).reshape(k // 512, 4)
    idx = np.arange(k)
    return np.exp2(a[idx // 512, idx % 128 // 32])


BF16 = ml_dtypes.bfloat16


def bf(x):
    return np.asarray(x, np.float32).astype(BF16)


def f64(x):
    return np.asarray(x).astype(np.float64)


H, N, D = 1, 2048, 128
DEG_P = 32.0 / N
NEG_SLOPE = 0.2
NEG = float(np.finfo(np.float32).min)


def setup_inputs():
    s = mx_kscale(N)
    r = s / s.min()
    L = np.log(r)
    x = bf(np.random.standard_normal((H, N, D)) * r[None, :, None])
    W = bf(np.random.standard_normal((H, N, D)) / np.sqrt(D) / r.max())
    b = bf(np.random.standard_normal((H, N)) * 0.3 + 1.5 * L.max() - L[None, :])
    neighbor_mask = (np.random.random((N, N)) < DEG_P) | np.eye(N, dtype=bool)
    return {"x": x, "W": W, "b": b, "neighbor_mask": neighbor_mask}


def reference(x, W, b, neighbor_mask):
    x = f64(x)
    m = np.asarray(neighbor_mask).astype(bool)[None]
    scores = x @ f64(W).transpose(0, 2, 1) + f64(b)[:, None, :]
    scores = np.where(scores >= 0.0, scores, NEG_SLOPE * scores)
    masked = np.where(m, scores, NEG)
    e = np.exp(masked - masked.max(-1, keepdims=True))
    att = e / e.sum(-1, keepdims=True)
    att = np.where(m, att, 0.0)
    return mxq(att, 2, "e4m3") @ mxq(x, 1, "e4m3")

@@ -1,0 +1,165 @@
+from contextlib import ExitStack
+
+import concourse.bass as bass
+import concourse.mybir as mybir
+import concourse.tile as tile
+from concourse.masks import make_identity
+
+F32 = mybir.dt.float32
+BF16 = mybir.dt.bfloat16
+I32 = mybir.dt.int32
+U32 = mybir.dt.uint32
+U8 = mybir.dt.uint8
+FP8X4 = mybir.dt.float8_e4m3fn_x4
+ALU = mybir.AluOpType
+ACT = mybir.ActivationFunctionType
+AX = mybir.AxisListType
+
+P = 128
+N = 2048
+D = 128
+G = 4
+F = 4
+FLOPS = 2 * 2 * N * N * D
+BIG = 2.0**125
+
+
+def tile_attention_kernel(tc, x, W, b, neighbor_mask, out):
+    nc = tc.nc
+    with ExitStack() as ctx:
+        keep = ctx.enter_context(tc.tile_pool(name="keep", bufs=1))
+        work = ctx.enter_context(tc.tile_pool(name="work", bufs=3))
+        maskp = ctx.enter_context(tc.tile_pool(name="maskp", bufs=3))
+        small = ctx.enter_context(tc.tile_pool(name="small", bufs=4))
+        ps_z = ctx.enter_context(tc.psum_pool(name="ps_z", bufs=4))
+        ps_t = ctx.enter_context(tc.psum_pool(name="ps_t", bufs=2))
+        ps_o = ctx.enter_context(tc.psum_pool(name="ps_o", bufs=2))
+
+        x_sb = keep.tile([P, G, F, D], BF16)
+        nc.sync.dma_start(
+            out=x_sb[:].rearrange("p g f d -> p g (f d)"),
+            in_=x[0].rearrange("(g p f) d -> p g (f d)", g=G, p=P, f=F),
+        )
+        w_sb = keep.tile([P, 8, 2, D], BF16)
+        nc.sync.dma_start(
+            out=w_sb[:].rearrange("r a h d -> r a (h d)"),
+            in_=W[0].rearrange("(a r h) d -> r a (h d)", a=8, r=P, h=2),
+        )
+        b_nat = keep.tile([P, N], BF16)
+        nc.scalar.dma_start(out=b_nat[:], in_=b[0].partition_broadcast(P))
+        mask_words = neighbor_mask.bitcast(I32).rearrange("(g p f) w -> p g f w", g=G, p=P, f=F)
+
+        ident_bf = keep.tile([P, P], BF16)
+        make_identity(nc, ident_bf[:])
+        ident_f = keep.tile([P, P], F32)
+        make_identity(nc, ident_f[:])
+
+        xT = keep.tile([P, G * F, P], BF16)
+        wT = keep.tile([P, 2, 8, P], BF16)
+        for q in range(4):
+            tp = ps_z.tile([P, 4, P], BF16, tag="z")
+            for k in range(4):
+                nc.tensor.transpose(tp[:, k, :], x_sb[:, q, k, :], ident_bf[:])
+            nc.vector.tensor_copy(out=xT[:, 4 * q : 4 * q + 4, :], in_=tp[:])
+        for h in range(2):
+            for q in range(2):
+                tp = ps_z.tile([P, 4, P], BF16, tag="z")
+                for k in range(4):
+                    nc.tensor.transpose(tp[:, k, :], w_sb[:, 4 * q + k, h, :], ident_bf[:])
+                nc.scalar.copy(out=wT[:, h, 4 * q : 4 * q + 4, :], in_=tp[:])
+        wT_flat = wT[:].rearrange("d h a r -> d (h a r)")
+
+        b_perm = keep.tile([P, 2, N // 2], BF16)
+        nc.vector.tensor_copy(out=b_perm[:], in_=b_nat[:].rearrange("p (c h) -> p h c", h=2))
+        b_flat = b_perm[:].rearrange("p h c -> p (h c)")
+
+        gx = keep.tile([P, G, D, 4], BF16, align_bytes=64)
+        for g in range(G):
+            nc.vector.tensor_copy(
+                out=gx[:, g, :, :].rearrange("p d (h e) -> p d h e", h=2),
+                in_=x_sb[:, g, :, :].rearrange("p (e h) d -> p d h e", h=2),
+            )
+        xq = keep.tile([P, G * D], U32, align_bytes=64)
+        xs = keep.tile([P, G * D], U8, align_bytes=64)
+        nc.vector.quantize_mx(
+            out=xq[:].bitcast(FP8X4), scales=xs[:], in_=gx[:].rearrange("p g d t -> p (g d t)")
+        )
+
+        out_rows = out[0].rearrange("(g p f) d -> p g (f d)", g=G, p=P, f=F)
+
+        for g in range(G):
+            o_sb = work.tile([P, F, D], F32, tag="o_sb", bufs=2)
+            for f in range(F):
+                it = g * F + f
+                m_t = maskp.tile([P, 2 * N], I32, tag="m_t")
+                nc.sync.dma_start(out=m_t[:], in_=mask_words[:, g, f, :])
+                pm = work.tile([P, 2, N // 2], BF16, tag="pm")
+                nc.vector.tensor_scalar(
+                    out=pm[:],
+                    in0=m_t[:].rearrange("p (c h two) -> p h c two", h=2, two=2)[:, :, :, 0],
+                    scalar1=-1.0, scalar2=BIG, op0=ALU.add, op1=ALU.mult,
+                )
+                bm = work.tile([P, N], BF16, tag="bm")
+                nc.vector.tensor_tensor(
+                    out=bm[:], in0=pm[:].rearrange("p h c -> p (h c)"), in1=b_flat, op=ALU.add
+                )
+
+                vm = work.tile([P, N], F32, tag="vm")
+                for k in range(4):
+                    z = ps_z.tile([P, 512], F32, tag="z")
+                    nc.tensor.matmul(
+                        out=z[:], lhsT=xT[:, it, :], rhs=wT_flat[:, 512 * k : 512 * k + 512],
+                        start=True, stop=True,
+                    )
+                    nc.vector.tensor_tensor(
+                        out=vm[:, 512 * k : 512 * k + 512], in0=z[:],
+                        in1=bm[:, 512 * k : 512 * k + 512], op=ALU.add,
+                    )
+                s = work.tile([P, N], F32, tag="s")
+                nc.vector.scalar_tensor_tensor(
+                    out=s[:], in0=vm[:], scalar=0.2, in1=vm[:], op0=ALU.mult, op1=ALU.max
+                )
+                negm = small.tile([P, 1], F32, tag="negm")
+                nc.vector.tensor_reduce(out=negm[:], in_=s[:], axis=AX.X, op=ALU.max, negate=True)
+                e = work.tile([P, N], F32, tag="e")
+                ssum = small.tile([P, 1], F32, tag="ssum")
+                nc.scalar.activation(
+                    out=e[:], in_=s[:], func=ACT.Exp, bias=negm[:], scale=1.0, accum_out=ssum[:]
+                )
+                rinv = small.tile([P, 1], F32, tag="rinv")
+                nc.vector.reciprocal(out=rinv[:], in_=ssum[:])
+                att = work.tile([P, N], BF16, tag="att")
+                nc.scalar.activation(out=att[:], in_=e[:], func=ACT.Copy, scale=rinv[:])
+                att_words = att[:].bitcast(F32)
+
+                grouped = work.tile([P, N], BF16, tag="grouped", align_bytes=64)
+                grouped_words = grouped[:].bitcast(F32).rearrange(
+                    "p (c i h) -> p c i h", c=G, i=P, h=2
+                )
+                for half in range(2):
+                    tp = ps_t.tile([P, 4, P], F32, tag="t")
+                    for c in range(2):
+                        for h in range(2):
+                            first = 512 * h + 128 * (2 * half + c)
+                            nc.tensor.transpose(
+                                tp[:, 2 * c + h, :], att_words[:, first : first + 128], ident_f[:]
+                            )
+                    nc.scalar.copy(
+                        out=grouped_words[:, 2 * half : 2 * half + 2, :, :],
+                        in_=tp[:].rearrange("p (c h) i -> p c i h", h=2),
+                    )
+                aq = work.tile([P, G * P], U32, tag="aq", align_bytes=64)
+                asc = work.tile([P, G * P], U8, tag="asc", align_bytes=64)
+                nc.vector.quantize_mx(out=aq[:].bitcast(FP8X4), scales=asc[:], in_=grouped[:])
+
+                o_ps = ps_o.tile([P, D], F32, tag="o")
+                for c in range(G):
+                    cols = slice(128 * c, 128 * c + 128)
+                    nc.tensor.matmul_mx(
+                        out=o_ps[:],
+                        lhsT=aq[:, cols].bitcast(FP8X4), lhsT_scale=asc[:, cols],
+                        rhs=xq[:, cols].bitcast(FP8X4), rhs_scale=xs[:, cols],
+                        start=(c == 0), stop=(c == G - 1),
+                    )
+                nc.scalar.copy(out=o_sb[:, f, :], in_=o_ps[:])
+            nc.scalar.dma_start(out=out_rows[:, g, :], in_=o_sb[:].rearrange("p f d -> p (f d)"))

@@ -1,8 +1,6 @@
 from contextlib import ExitStack
 
-import concourse.bass as bass
 import concourse.mybir as mybir
-import concourse.tile as tile
 from concourse.masks import make_identity
 
 F32 = mybir.dt.float32
@@ -19,147 +17,268 @@ P = 128
 N = 2048
 D = 128
 G = 4
-F = 4
+T = N // P
 FLOPS = 2 * 2 * N * N * D
 BIG = 2.0**125
+NORM = "gpsimd"
+CONV_V_COLS = 0
 
 
 def tile_attention_kernel(tc, x, W, b, neighbor_mask, out):
     nc = tc.nc
     with ExitStack() as ctx:
+        ctx.enter_context(tc.manual_schedule())
         keep = ctx.enter_context(tc.tile_pool(name="keep", bufs=1))
-        work = ctx.enter_context(tc.tile_pool(name="work", bufs=3))
+        work = ctx.enter_context(tc.tile_pool(name="work", bufs=2))
         maskp = ctx.enter_context(tc.tile_pool(name="maskp", bufs=3))
         small = ctx.enter_context(tc.tile_pool(name="small", bufs=4))
         ps_z = ctx.enter_context(tc.psum_pool(name="ps_z", bufs=4))
         ps_t = ctx.enter_context(tc.psum_pool(name="ps_t", bufs=2))
         ps_o = ctx.enter_context(tc.psum_pool(name="ps_o", bufs=2))
 
-        x_sb = keep.tile([P, G, F, D], BF16)
-        nc.sync.dma_start(
-            out=x_sb[:].rearrange("p g f d -> p g (f d)"),
-            in_=x[0].rearrange("(g p f) d -> p g (f d)", g=G, p=P, f=F),
-        )
-        w_sb = keep.tile([P, 8, 2, D], BF16)
-        nc.sync.dma_start(
-            out=w_sb[:].rearrange("r a h d -> r a (h d)"),
-            in_=W[0].rearrange("(a r h) d -> r a (h d)", a=8, r=P, h=2),
-        )
-        b_nat = keep.tile([P, N], BF16)
-        nc.scalar.dma_start(out=b_nat[:], in_=b[0].partition_broadcast(P))
-        mask_words = neighbor_mask.bitcast(I32).rearrange("(g p f) w -> p g f w", g=G, p=P, f=F)
+        mask_words = neighbor_mask.bitcast(I32).rearrange("(q p e) w -> p q e w", q=8, p=P, e=2)
+        out_rows = out[0].rearrange("(q p e) d -> p q (e d)", q=8, p=P, e=2)
+        w_rows = W[0].rearrange("(k p) d -> p k d", p=P)
+        st = {}
+
+        def load_mask(t, first, last):
+            if first == 0:
+                st[("m", t)] = maskp.tile([P, 2 * N], I32, tag="m_t", name="m_t")
+            nc.sync.dma_start(
+                out=st[("m", t)][:, 2 * first : 2 * last],
+                in_=mask_words[:, t // 2, t % 2, 2 * first : 2 * last],
+            )
+
+        b16 = keep.tile([P, P], BF16)
+        nc.gpsimd.memset(b16[:], 0.0)
+        nc.scalar.dma_start(out=b16[0:16, :], in_=b[0].rearrange("(r c) -> r c", c=P))
+        x_sb = keep.tile([P, T, D], BF16)
+        x_dst = x_sb[:].rearrange("p (q e) d -> p q (e d)", e=2)
+        x_src = x[0].rearrange("(q p e) d -> p q (e d)", q=8, p=P, e=2)
+        w_sb = keep.tile([P, T, D], BF16)
+        for k in range(4):
+            nc.sync.dma_start(out=w_sb[:, 4 * k : 4 * k + 4, :], in_=w_rows[:, 4 * k : 4 * k + 4, :])
+            if k == 0:
+                nc.sync.dma_start(out=x_dst[:, 0:2, :], in_=x_src[:, 0:2, :])
+            load_mask(0, 512 * k, 512 * k + 512)
+        nc.sync.dma_start(out=x_dst[:, 2:8, :], in_=x_src[:, 2:8, :])
+        load_mask(1, 0, N)
 
         ident_bf = keep.tile([P, P], BF16)
         make_identity(nc, ident_bf[:])
         ident_f = keep.tile([P, P], F32)
         make_identity(nc, ident_f[:])
 
-        xT = keep.tile([P, G * F, P], BF16)
-        wT = keep.tile([P, 2, 8, P], BF16)
-        for q in range(4):
-            tp = ps_z.tile([P, 4, P], BF16, tag="z")
-            for k in range(4):
-                nc.tensor.transpose(tp[:, k, :], x_sb[:, q, k, :], ident_bf[:])
-            nc.vector.tensor_copy(out=xT[:, 4 * q : 4 * q + 4, :], in_=tp[:])
-        for h in range(2):
-            for q in range(2):
-                tp = ps_z.tile([P, 4, P], BF16, tag="z")
-                for k in range(4):
-                    nc.tensor.transpose(tp[:, k, :], w_sb[:, 4 * q + k, h, :], ident_bf[:])
-                nc.scalar.copy(out=wT[:, h, 4 * q : 4 * q + 4, :], in_=tp[:])
-        wT_flat = wT[:].rearrange("d h a r -> d (h a r)")
-
-        b_perm = keep.tile([P, 2, N // 2], BF16)
-        nc.vector.tensor_copy(out=b_perm[:], in_=b_nat[:].rearrange("p (c h) -> p h c", h=2))
-        b_flat = b_perm[:].rearrange("p h c -> p (h c)")
-
+        xT = keep.tile([P, T, P], BF16)
+        wT = keep.tile([P, T, P], BF16)
+        bcol = keep.tile([P, T], F32)
         gx = keep.tile([P, G, D, 4], BF16, align_bytes=64)
-        for g in range(G):
-            nc.vector.tensor_copy(
-                out=gx[:, g, :, :].rearrange("p d (h e) -> p d h e", h=2),
-                in_=x_sb[:, g, :, :].rearrange("p (e h) d -> p d h e", h=2),
-            )
         xq = keep.tile([P, G * D], U32, align_bytes=64)
         xs = keep.tile([P, G * D], U8, align_bytes=64)
-        nc.vector.quantize_mx(
-            out=xq[:].bitcast(FP8X4), scales=xs[:], in_=gx[:].rearrange("p g d t -> p (g d t)")
-        )
 
-        out_rows = out[0].rearrange("(g p f) d -> p g (f d)", g=G, p=P, f=F)
+        def flip(dst, src, q, engine):
+            tp = ps_t.tile([P, 4, P], BF16, tag="t", name="tpb")
+            for k in range(4):
+                nc.tensor.transpose(tp[:, k, :], src[:, 4 * q + k, :], ident_bf[:])
+            if engine == "vector":
+                nc.vector.tensor_copy(out=dst[:, 4 * q : 4 * q + 4, :], in_=tp[:])
+            else:
+                nc.scalar.copy(out=dst[:, 4 * q : 4 * q + 4, :], in_=tp[:])
 
-        for g in range(G):
-            o_sb = work.tile([P, F, D], F32, tag="o_sb", bufs=2)
-            for f in range(F):
-                it = g * F + f
-                m_t = maskp.tile([P, 2 * N], I32, tag="m_t")
-                nc.sync.dma_start(out=m_t[:], in_=mask_words[:, g, f, :])
-                pm = work.tile([P, 2, N // 2], BF16, tag="pm")
+        def conv(t, first, last, engine):
+            if first == 0:
+                st[("pm", t)] = work.tile([P, N], BF16, tag="pm", name="pm")
+            pm = st[("pm", t)]
+            m_t = st[("m", t)]
+            if engine == "vector":
                 nc.vector.tensor_scalar(
-                    out=pm[:],
-                    in0=m_t[:].rearrange("p (c h two) -> p h c two", h=2, two=2)[:, :, :, 0],
+                    out=pm[:, first:last],
+                    in0=m_t[:].rearrange("p (j two) -> p j two", two=2)[:, first:last, 0],
                     scalar1=-1.0, scalar2=BIG, op0=ALU.add, op1=ALU.mult,
                 )
-                bm = work.tile([P, N], BF16, tag="bm")
-                nc.vector.tensor_tensor(
-                    out=bm[:], in0=pm[:].rearrange("p h c -> p (h c)"), in1=b_flat, op=ALU.add
-                )
-
-                vm = work.tile([P, N], F32, tag="vm")
-                for k in range(4):
-                    z = ps_z.tile([P, 512], F32, tag="z")
-                    nc.tensor.matmul(
-                        out=z[:], lhsT=xT[:, it, :], rhs=wT_flat[:, 512 * k : 512 * k + 512],
-                        start=True, stop=True,
-                    )
-                    nc.vector.tensor_tensor(
-                        out=vm[:, 512 * k : 512 * k + 512], in0=z[:],
-                        in1=bm[:, 512 * k : 512 * k + 512], op=ALU.add,
-                    )
-                s = work.tile([P, N], F32, tag="s")
-                nc.vector.scalar_tensor_tensor(
-                    out=s[:], in0=vm[:], scalar=0.2, in1=vm[:], op0=ALU.mult, op1=ALU.max
-                )
-                negm = small.tile([P, 1], F32, tag="negm")
-                nc.vector.tensor_reduce(out=negm[:], in_=s[:], axis=AX.X, op=ALU.max, negate=True)
-                e = work.tile([P, N], F32, tag="e")
-                ssum = small.tile([P, 1], F32, tag="ssum")
+            else:
                 nc.scalar.activation(
-                    out=e[:], in_=s[:], func=ACT.Exp, bias=negm[:], scale=1.0, accum_out=ssum[:]
+                    out=pm[:, first:last],
+                    in_=m_t[:].bitcast(U32).rearrange("p (j two) -> p j two", two=2)[:, first:last, 0],
+                    func=ACT.Copy, scale=BIG, bias=-BIG,
                 )
-                rinv = small.tile([P, 1], F32, tag="rinv")
-                nc.vector.reciprocal(out=rinv[:], in_=ssum[:])
-                att = work.tile([P, N], BF16, tag="att")
-                nc.scalar.activation(out=att[:], in_=e[:], func=ACT.Copy, scale=rinv[:])
-                att_words = att[:].bitcast(F32)
 
-                grouped = work.tile([P, N], BF16, tag="grouped", align_bytes=64)
-                grouped_words = grouped[:].bitcast(F32).rearrange(
-                    "p (c i h) -> p c i h", c=G, i=P, h=2
+        def scores(t, k):
+            z = ps_z.tile([P, 512], F32, tag="z", name="z")
+            for q in range(4):
+                kb = 4 * k + q
+                cols = slice(128 * q, 128 * q + 128)
+                nc.tensor.matmul(
+                    out=z[:, cols], lhsT=xT[:, t, :], rhs=wT[:, kb, :], start=True, stop=False
                 )
-                for half in range(2):
-                    tp = ps_t.tile([P, 4, P], F32, tag="t")
-                    for c in range(2):
-                        for h in range(2):
-                            first = 512 * h + 128 * (2 * half + c)
-                            nc.tensor.transpose(
-                                tp[:, 2 * c + h, :], att_words[:, first : first + 128], ident_f[:]
-                            )
+                nc.tensor.matmul(
+                    out=z[:, cols], lhsT=bcol[:, kb : kb + 1].to_broadcast([P, P]),
+                    rhs=ident_f[:], is_transpose=True, start=False, stop=True,
+                )
+            st[("z", t, k)] = z
+
+        def add_mask(t, k):
+            if k == 0:
+                st[("vm", t)] = work.tile([P, N], F32, tag="vm", name="vm")
+            cols = slice(512 * k, 512 * k + 512)
+            nc.vector.tensor_tensor(
+                out=st[("vm", t)][:, cols], in0=st[("z", t, k)][:], in1=st[("pm", t)][:, cols],
+                op=ALU.add,
+            )
+
+        def leaky(t):
+            vm = st[("vm", t)]
+            s = work.tile([P, N], F32, tag="s", name="s")
+            for h in range(2):
+                cols = slice(1024 * h, 1024 * h + 1024)
+                nc.vector.scalar_tensor_tensor(
+                    out=s[:, cols], in0=vm[:, cols], scalar=0.2, in1=vm[:, cols],
+                    op0=ALU.mult, op1=ALU.max,
+                )
+            st[("s", t)] = s
+
+        def row_max(t):
+            negm = small.tile([P, 1], F32, tag="negm", name="negm")
+            nc.vector.tensor_reduce(
+                out=negm[:], in_=st[("s", t)][:], axis=AX.X, op=ALU.max, negate=True
+            )
+            st[("negm", t)] = negm
+
+        def exp_sum(t):
+            e = work.tile([P, N], F32, tag="e", name="e")
+            ssum = small.tile([P, 1], F32, tag="ssum", name="ssum")
+            nc.scalar.activation(
+                out=e[:], in_=st[("s", t)][:], func=ACT.Exp, bias=st[("negm", t)][:], scale=1.0,
+                accum_out=ssum[:],
+            )
+            st[("e", t)] = e
+            st[("ssum", t)] = ssum
+
+        def normalise(t, engine):
+            rinv = small.tile([P, 1], F32, tag="rinv", name="rinv")
+            nc.vector.reciprocal(out=rinv[:], in_=st[("ssum", t)][:])
+            att = work.tile([P, N], BF16, tag="att", name="att")
+            if engine == "gpsimd":
+                nc.gpsimd.tensor_scalar(
+                    out=att[:], in0=st[("e", t)][:], scalar1=rinv[:], scalar2=0.0,
+                    op0=ALU.mult, op1=ALU.add,
+                )
+            elif engine == "vector":
+                nc.vector.tensor_scalar(
+                    out=att[:], in0=st[("e", t)][:], scalar1=rinv[:], scalar2=None, op0=ALU.mult
+                )
+            else:
+                nc.scalar.activation(out=att[:], in_=st[("e", t)][:], func=ACT.Copy, scale=rinv[:])
+            st[("att", t)] = att
+
+        def transpose_att(t):
+            att_words = st[("att", t)][:].bitcast(F32)
+            grouped = work.tile([P, N], BF16, tag="grouped", name="grouped", align_bytes=64)
+            grouped_words = grouped[:].bitcast(F32).rearrange("p (c i u) -> p c i u", c=G, i=P, u=2)
+            for half in range(2):
+                tp = ps_t.tile([P, 4, P], F32, tag="t", name="tp")
+                for k in range(4):
+                    first = 128 * (4 * half + k)
+                    nc.tensor.transpose(tp[:, k, :], att_words[:, first : first + 128], ident_f[:])
+                nc.scalar.copy(
+                    out=grouped_words[:, 2 * half : 2 * half + 2, :, :],
+                    in_=tp[:].rearrange("p (c u) i -> p c i u", u=2),
+                )
+            st[("grouped", t)] = grouped
+
+        def quantise(t):
+            aq = work.tile([P, G * P], U32, tag="aq", name="aq", align_bytes=64)
+            asc = work.tile([P, G * P], U8, tag="asc", name="asc", align_bytes=64)
+            nc.vector.quantize_mx(
+                out=aq[:].bitcast(FP8X4), scales=asc[:], in_=st[("grouped", t)][:]
+            )
+            st[("aq", t)] = aq
+            st[("asc", t)] = asc
+
+        def multiply(t):
+            aq = st[("aq", t)]
+            asc = st[("asc", t)]
+            o_ps = ps_o.tile([P, D], F32, tag="o", name="o_ps")
+            for c in range(G):
+                cols = slice(128 * c, 128 * c + 128)
+                nc.tensor.matmul_mx(
+                    out=o_ps[:],
+                    lhsT=aq[:, cols].bitcast(FP8X4), lhsT_scale=asc[:, cols],
+                    rhs=xq[:, cols].bitcast(FP8X4), rhs_scale=xs[:, cols],
+                    start=(c == 0), stop=(c == G - 1),
+                )
+            st[("o", t)] = o_ps
+
+        def store(t):
+            if t % 2 == 0:
+                st["o_sb"] = work.tile([P, 2, D], F32, tag="o_sb", name="o_sb")
+            o_sb = st["o_sb"]
+            nc.scalar.copy(out=o_sb[:, t % 2, :], in_=st[("o", t)][:])
+            if t % 2 == 1:
+                nc.sync.dma_start(
+                    out=out_rows[:, t // 2, :], in_=o_sb[:].rearrange("p e d -> p (e d)")
+                )
+
+        flip(wT, w_sb, 0, "scalar")
+        flip(xT, x_sb, 0, "vector")
+        tb = ps_t.tile([P, P], BF16, tag="t")
+        nc.tensor.transpose(tb[:], b16[:], ident_bf[:])
+        nc.vector.tensor_copy(out=bcol[:], in_=tb[:, 0:T])
+        scores(0, 0)
+        for k in range(1, 4):
+            flip(wT, w_sb, k, "scalar")
+            scores(0, k)
+        for q in range(1, 4):
+            flip(xT, x_sb, q, "scalar")
+
+        for t in range(T):
+            if t + 2 < T:
+                load_mask(t + 2, 0, N)
+            if t - 2 >= 0:
+                normalise(t - 2, NORM)
+            if t - 1 >= 0:
+                exp_sum(t - 1)
+            for k in range(4):
+                if t == 0:
+                    conv(0, 512 * k, 512 * k + 512, "vector")
+                add_mask(t, k)
+                if t + 1 < T:
+                    scores(t + 1, k)
+            if t + 1 < T:
+                conv(t + 1, 0, N - CONV_V_COLS, "scalar")
+            if t == 0:
+                for g in range(G):
                     nc.scalar.copy(
-                        out=grouped_words[:, 2 * half : 2 * half + 2, :, :],
-                        in_=tp[:].rearrange("p (c h) i -> p c i h", h=2),
+                        out=gx[:, g, :, :],
+                        in_=x_sb[:, 4 * g : 4 * g + 4, :].rearrange("p t d -> p d t"),
                     )
-                aq = work.tile([P, G * P], U32, tag="aq", align_bytes=64)
-                asc = work.tile([P, G * P], U8, tag="asc", align_bytes=64)
-                nc.vector.quantize_mx(out=aq[:].bitcast(FP8X4), scales=asc[:], in_=grouped[:])
+            if t - 2 >= 0:
+                transpose_att(t - 2)
+            leaky(t)
+            if t - 3 >= 0:
+                quantise(t - 3)
+                multiply(t - 3)
+                store(t - 3)
+            if t == 1:
+                nc.vector.quantize_mx(
+                    out=xq[:].bitcast(FP8X4), scales=xs[:],
+                    in_=gx[:].rearrange("p g d t -> p (g d t)"),
+                )
+            if t + 1 < T and CONV_V_COLS > 0:
+                conv(t + 1, N - CONV_V_COLS, N, "vector")
+            row_max(t)
 
-                o_ps = ps_o.tile([P, D], F32, tag="o")
-                for c in range(G):
-                    cols = slice(128 * c, 128 * c + 128)
-                    nc.tensor.matmul_mx(
-                        out=o_ps[:],
-                        lhsT=aq[:, cols].bitcast(FP8X4), lhsT_scale=asc[:, cols],
-                        rhs=xq[:, cols].bitcast(FP8X4), rhs_scale=xs[:, cols],
-                        start=(c == 0), stop=(c == G - 1),
-                    )
-                nc.scalar.copy(out=o_sb[:, f, :], in_=o_ps[:])
-            nc.scalar.dma_start(out=out_rows[:, g, :], in_=o_sb[:].rearrange("p f d -> p (f d)"))
+        normalise(T - 2, "vector")
+        exp_sum(T - 1)
+        quantise(T - 3)
+        multiply(T - 3)
+        transpose_att(T - 2)
+        store(T - 3)
+        normalise(T - 1, "vector")
+        quantise(T - 2)
+        transpose_att(T - 1)
+        multiply(T - 2)
+        store(T - 2)
+        quantise(T - 1)
+        multiply(T - 1)
+        store(T - 1)

@@ -20,14 +20,11 @@ G = 4
 T = N // P
 FLOPS = 2 * 2 * N * N * D
 BIG = 2.0**125
-NORM = "gpsimd"
-CONV_V_COLS = 0
 
 
 def tile_attention_kernel(tc, x, W, b, neighbor_mask, out):
     nc = tc.nc
     with ExitStack() as ctx:
-        ctx.enter_context(tc.manual_schedule())
         keep = ctx.enter_context(tc.tile_pool(name="keep", bufs=1))
         work = ctx.enter_context(tc.tile_pool(name="work", bufs=2))
         maskp = ctx.enter_context(tc.tile_pool(name="maskp", bufs=3))
@@ -41,6 +38,18 @@ def tile_attention_kernel(tc, x, W, b, neighbor_mask, out):
         w_rows = W[0].rearrange("(k p) d -> p k d", p=P)
         st = {}
 
+        xT = keep.tile([P, T, P], BF16)
+        wT = keep.tile([P, T, P], BF16)
+        bcol = keep.tile([P, T], F32)
+        gx = keep.tile([P, G, D, 4], BF16, align_bytes=64)
+        xq = keep.tile([P, G * D], U32, align_bytes=64)
+        xs = keep.tile([P, G * D], U8, align_bytes=64)
+        b16 = keep.tile([P, P], BF16)
+        x_sb = keep.tile([P, T, D], BF16)
+        w_sb = keep.tile([P, T, D], BF16)
+        ident_bf = keep.tile([P, P], BF16)
+        ident_f = keep.tile([P, P], F32)
+
         def load_mask(t, first, last):
             if first == 0:
                 st[("m", t)] = maskp.tile([P, 2 * N], I32, tag="m_t", name="m_t")
@@ -48,33 +57,6 @@ def tile_attention_kernel(tc, x, W, b, neighbor_mask, out):
                 out=st[("m", t)][:, 2 * first : 2 * last],
                 in_=mask_words[:, t // 2, t % 2, 2 * first : 2 * last],
             )
-
-        b16 = keep.tile([P, P], BF16)
-        nc.gpsimd.memset(b16[:], 0.0)
-        nc.scalar.dma_start(out=b16[0:16, :], in_=b[0].rearrange("(r c) -> r c", c=P))
-        x_sb = keep.tile([P, T, D], BF16)
-        x_dst = x_sb[:].rearrange("p (q e) d -> p q (e d)", e=2)
-        x_src = x[0].rearrange("(q p e) d -> p q (e d)", q=8, p=P, e=2)
-        w_sb = keep.tile([P, T, D], BF16)
-        for k in range(4):
-            nc.sync.dma_start(out=w_sb[:, 4 * k : 4 * k + 4, :], in_=w_rows[:, 4 * k : 4 * k + 4, :])
-            if k == 0:
-                nc.sync.dma_start(out=x_dst[:, 0:2, :], in_=x_src[:, 0:2, :])
-            load_mask(0, 512 * k, 512 * k + 512)
-        nc.sync.dma_start(out=x_dst[:, 2:8, :], in_=x_src[:, 2:8, :])
-        load_mask(1, 0, N)
-
-        ident_bf = keep.tile([P, P], BF16)
-        make_identity(nc, ident_bf[:])
-        ident_f = keep.tile([P, P], F32)
-        make_identity(nc, ident_f[:])
-
-        xT = keep.tile([P, T, P], BF16)
-        wT = keep.tile([P, T, P], BF16)
-        bcol = keep.tile([P, T], F32)
-        gx = keep.tile([P, G, D, 4], BF16, align_bytes=64)
-        xq = keep.tile([P, G * D], U32, align_bytes=64)
-        xs = keep.tile([P, G * D], U8, align_bytes=64)
 
         def flip(dst, src, q, engine):
             tp = ps_t.tile([P, 4, P], BF16, tag="t", name="tpb")
@@ -87,7 +69,7 @@ def tile_attention_kernel(tc, x, W, b, neighbor_mask, out):
 
         def conv(t, first, last, engine):
             if first == 0:
-                st[("pm", t)] = work.tile([P, N], BF16, tag="pm", name="pm")
+                st[("pm", t)] = work.tile([P, N], BF16, tag="pm", name="pm", bufs=3)
             pm = st[("pm", t)]
             m_t = st[("m", t)]
             if engine == "vector":
@@ -145,7 +127,7 @@ def tile_attention_kernel(tc, x, W, b, neighbor_mask, out):
             st[("negm", t)] = negm
 
         def exp_sum(t):
-            e = work.tile([P, N], F32, tag="e", name="e")
+            e = work.tile([P, N], F32, tag="e", name="e", bufs=3)
             ssum = small.tile([P, 1], F32, tag="ssum", name="ssum")
             nc.scalar.activation(
                 out=e[:], in_=st[("s", t)][:], func=ACT.Exp, bias=st[("negm", t)][:], scale=1.0,
@@ -163,27 +145,31 @@ def tile_attention_kernel(tc, x, W, b, neighbor_mask, out):
                     out=att[:], in0=st[("e", t)][:], scalar1=rinv[:], scalar2=0.0,
                     op0=ALU.mult, op1=ALU.add,
                 )
-            elif engine == "vector":
+            else:
                 nc.vector.tensor_scalar(
                     out=att[:], in0=st[("e", t)][:], scalar1=rinv[:], scalar2=None, op0=ALU.mult
                 )
-            else:
-                nc.scalar.activation(out=att[:], in_=st[("e", t)][:], func=ACT.Copy, scale=rinv[:])
             st[("att", t)] = att
 
-        def transpose_att(t):
+        def transpose_att(t, engines=("scalar", "scalar")):
             att_words = st[("att", t)][:].bitcast(F32)
-            grouped = work.tile([P, N], BF16, tag="grouped", name="grouped", align_bytes=64)
+            grouped = work.tile([P, N], BF16, tag="grouped", name="grouped", align_bytes=64, bufs=4)
             grouped_words = grouped[:].bitcast(F32).rearrange("p (c i u) -> p c i u", c=G, i=P, u=2)
             for half in range(2):
                 tp = ps_t.tile([P, 4, P], F32, tag="t", name="tp")
                 for k in range(4):
                     first = 128 * (4 * half + k)
                     nc.tensor.transpose(tp[:, k, :], att_words[:, first : first + 128], ident_f[:])
-                nc.scalar.copy(
-                    out=grouped_words[:, 2 * half : 2 * half + 2, :, :],
-                    in_=tp[:].rearrange("p (c u) i -> p c i u", u=2),
-                )
+                if engines[half] == "scalar":
+                    nc.scalar.copy(
+                        out=grouped_words[:, 2 * half : 2 * half + 2, :, :],
+                        in_=tp[:].rearrange("p (c u) i -> p c i u", u=2),
+                    )
+                else:
+                    nc.vector.tensor_copy(
+                        out=grouped_words[:, 2 * half : 2 * half + 2, :, :],
+                        in_=tp[:].rearrange("p (c u) i -> p c i u", u=2),
+                    )
             st[("grouped", t)] = grouped
 
         def quantise(t):
@@ -219,66 +205,82 @@ def tile_attention_kernel(tc, x, W, b, neighbor_mask, out):
                     out=out_rows[:, t // 2, :], in_=o_sb[:].rearrange("p e d -> p (e d)")
                 )
 
-        flip(wT, w_sb, 0, "scalar")
-        flip(xT, x_sb, 0, "vector")
-        tb = ps_t.tile([P, P], BF16, tag="t")
-        nc.tensor.transpose(tb[:], b16[:], ident_bf[:])
-        nc.vector.tensor_copy(out=bcol[:], in_=tb[:, 0:T])
-        scores(0, 0)
-        for k in range(1, 4):
-            flip(wT, w_sb, k, "scalar")
-            scores(0, k)
-        for q in range(1, 4):
-            flip(xT, x_sb, q, "scalar")
-
-        for t in range(T):
-            if t + 2 < T:
-                load_mask(t + 2, 0, N)
-            if t - 2 >= 0:
-                normalise(t - 2, NORM)
-            if t - 1 >= 0:
-                exp_sum(t - 1)
+        with tc.manual_schedule():
+            nc.gpsimd.memset(b16[:], 0.0)
+            nc.scalar.dma_start(out=b16[0:16, :], in_=b[0].rearrange("(r c) -> r c", c=P))
+            x_dst = x_sb[:].rearrange("p (q e) d -> p q (e d)", e=2)
+            x_src = x[0].rearrange("(q p e) d -> p q (e d)", q=8, p=P, e=2)
             for k in range(4):
-                if t == 0:
-                    conv(0, 512 * k, 512 * k + 512, "vector")
-                add_mask(t, k)
-                if t + 1 < T:
-                    scores(t + 1, k)
-            if t + 1 < T:
-                conv(t + 1, 0, N - CONV_V_COLS, "scalar")
-            if t == 0:
-                for g in range(G):
-                    nc.scalar.copy(
-                        out=gx[:, g, :, :],
-                        in_=x_sb[:, 4 * g : 4 * g + 4, :].rearrange("p t d -> p d t"),
-                    )
-            if t - 2 >= 0:
-                transpose_att(t - 2)
-            leaky(t)
-            if t - 3 >= 0:
-                quantise(t - 3)
-                multiply(t - 3)
-                store(t - 3)
-            if t == 1:
-                nc.vector.quantize_mx(
-                    out=xq[:].bitcast(FP8X4), scales=xs[:],
-                    in_=gx[:].rearrange("p g d t -> p (g d t)"),
+                nc.sync.dma_start(
+                    out=w_sb[:, 4 * k : 4 * k + 4, :], in_=w_rows[:, 4 * k : 4 * k + 4, :]
                 )
-            if t + 1 < T and CONV_V_COLS > 0:
-                conv(t + 1, N - CONV_V_COLS, N, "vector")
-            row_max(t)
+                if k == 0:
+                    nc.sync.dma_start(out=x_dst[:, 0:2, :], in_=x_src[:, 0:2, :])
+                load_mask(0, 512 * k, 512 * k + 512)
+            for k in range(4):
+                load_mask(1, 512 * k, 512 * k + 512)
+            nc.sync.dma_start(out=x_dst[:, 2:8, :], in_=x_src[:, 2:8, :])
+            load_mask(2, 0, N)
+            make_identity(nc, ident_bf[:])
+            make_identity(nc, ident_f[:])
 
-        normalise(T - 2, "vector")
-        exp_sum(T - 1)
-        quantise(T - 3)
-        multiply(T - 3)
-        transpose_att(T - 2)
-        store(T - 3)
-        normalise(T - 1, "vector")
-        quantise(T - 2)
-        transpose_att(T - 1)
-        multiply(T - 2)
-        store(T - 2)
-        quantise(T - 1)
-        multiply(T - 1)
-        store(T - 1)
+            flip(wT, w_sb, 0, "scalar")
+            flip(xT, x_sb, 0, "vector")
+            tb = ps_t.tile([P, P], BF16, tag="t")
+            nc.tensor.transpose(tb[:], b16[:], ident_bf[:])
+            nc.vector.tensor_copy(out=bcol[:], in_=tb[:, 0:T])
+            scores(0, 0)
+            for k in range(1, 4):
+                flip(wT, w_sb, k, "scalar")
+                scores(0, k)
+            for k in range(4):
+                conv(1, 512 * k, 512 * k + 512, "scalar")
+
+            for u in range(T):
+                if u + 3 < T:
+                    load_mask(u + 3, 0, N)
+                if u - 1 >= 0:
+                    exp_sum(u - 1)
+                if u - 3 >= 0:
+                    transpose_att(u - 3)
+                for k in range(4):
+                    if u == 0:
+                        conv(0, 512 * k, 512 * k + 512, "vector")
+                    add_mask(u, k)
+                    if u + 1 < T:
+                        scores(u + 1, k)
+                if u == 0:
+                    for q in range(1, 4):
+                        flip(xT, x_sb, q, "scalar")
+                if 1 <= u and u + 1 < T:
+                    conv(u + 1, 0, N, "scalar")
+                if u == 0:
+                    for g in range(G):
+                        nc.scalar.copy(
+                            out=gx[:, g, :, :],
+                            in_=x_sb[:, 4 * g : 4 * g + 4, :].rearrange("p t d -> p d t"),
+                        )
+                leaky(u)
+                if u - 4 >= 0:
+                    quantise(u - 4)
+                    multiply(u - 4)
+                    store(u - 4)
+                if u == 1:
+                    nc.vector.quantize_mx(
+                        out=xq[:].bitcast(FP8X4), scales=xs[:],
+                        in_=gx[:].rearrange("p g d t -> p (g d t)"),
+                    )
+                if u - 2 >= 0:
+                    normalise(u - 2, "gpsimd")
+                row_max(u)
+
+            exp_sum(T - 1)
+            normalise(T - 2, "vector")
+            transpose_att(T - 3, ("vector", "vector"))
+            transpose_att(T - 2)
+            normalise(T - 1, "vector")
+            transpose_att(T - 1)
+            for t in range(T - 4, T):
+                quantise(t)
+                multiply(t)
+                store(t)

@@ -29,7 +29,8 @@ def tile_attention_kernel(tc, x, W, b, neighbor_mask, out):
         work = ctx.enter_context(tc.tile_pool(name="work", bufs=2))
         maskp = ctx.enter_context(tc.tile_pool(name="maskp", bufs=3))
         small = ctx.enter_context(tc.tile_pool(name="small", bufs=4))
-        ps_z = ctx.enter_context(tc.psum_pool(name="ps_z", bufs=4))
+        ps_z = ctx.enter_context(tc.psum_pool(name="ps_z", bufs=3))
+        ps_z3 = ctx.enter_context(tc.psum_pool(name="ps_z3", bufs=1))
         ps_t = ctx.enter_context(tc.psum_pool(name="ps_t", bufs=2))
         ps_o = ctx.enter_context(tc.psum_pool(name="ps_o", bufs=2))
 
@@ -86,7 +87,10 @@ def tile_attention_kernel(tc, x, W, b, neighbor_mask, out):
                 )
 
         def scores(t, k):
-            z = ps_z.tile([P, 512], F32, tag="z", name="z")
+            if k < 3:
+                z = ps_z.tile([P, 512], F32, tag="z", name="z")
+            else:
+                z = ps_z3.tile([P, 512], F32, tag="z3", name="z3")
             for q in range(4):
                 kb = 4 * k + q
                 cols = slice(128 * q, 128 * q + 128)
@@ -99,9 +103,22 @@ def tile_attention_kernel(tc, x, W, b, neighbor_mask, out):
                 )
             st[("z", t, k)] = z
 
+        def new_vm(t):
+            st[("vm", t)] = work.tile([P, N], F32, tag="vm", name="vm")
+
+        def fetch_last_bank(t):
+            zb = work.tile([P, 512], F32, tag="zb", name="zb")
+            nc.scalar.copy(out=zb[:], in_=st[("z", t, 3)][:])
+            st[("zb", t)] = zb
+
+        def add_mask_last_bank(t):
+            new_vm(t)
+            nc.gpsimd.tensor_tensor(
+                out=st[("vm", t)][:, 1536:2048], in0=st[("zb", t)][:],
+                in1=st[("pm", t)][:, 1536:2048], op=ALU.add,
+            )
+
         def add_mask(t, k):
-            if k == 0:
-                st[("vm", t)] = work.tile([P, N], F32, tag="vm", name="vm")
             cols = slice(512 * k, 512 * k + 512)
             nc.vector.tensor_tensor(
                 out=st[("vm", t)][:, cols], in0=st[("z", t, k)][:], in1=st[("pm", t)][:, cols],
@@ -235,6 +252,7 @@ def tile_attention_kernel(tc, x, W, b, neighbor_mask, out):
                 scores(0, k)
             for k in range(4):
                 conv(1, 512 * k, 512 * k + 512, "scalar")
+            new_vm(0)
 
             for u in range(T):
                 if u + 3 < T:
@@ -243,17 +261,24 @@ def tile_attention_kernel(tc, x, W, b, neighbor_mask, out):
                     exp_sum(u - 1)
                 if u - 3 >= 0:
                     transpose_att(u - 3)
-                for k in range(4):
+                if 1 <= u and u + 1 < T:
+                    scores(u + 1, 3)
+                for k in range(3):
                     if u == 0:
                         conv(0, 512 * k, 512 * k + 512, "vector")
                     add_mask(u, k)
                     if u + 1 < T:
                         scores(u + 1, k)
                 if u == 0:
+                    conv(0, 1536, 2048, "vector")
+                    add_mask(0, 3)
+                    scores(1, 3)
                     for q in range(1, 4):
                         flip(xT, x_sb, q, "scalar")
                 if 1 <= u and u + 1 < T:
                     conv(u + 1, 0, N, "scalar")
+                if u + 1 < T:
+                    fetch_last_bank(u + 1)
                 if u == 0:
                     for g in range(G):
                         nc.scalar.copy(
@@ -272,6 +297,8 @@ def tile_attention_kernel(tc, x, W, b, neighbor_mask, out):
                     )
                 if u - 2 >= 0:
                     normalise(u - 2, "gpsimd")
+                if u + 1 < T:
+                    add_mask_last_bank(u + 1)
                 row_max(u)
 
             exp_sum(T - 1)

@@ -237,7 +237,8 @@ def tile_attention_kernel(tc, x, W, b, neighbor_mask, out):
             for k in range(4):
                 load_mask(1, 512 * k, 512 * k + 512)
             nc.sync.dma_start(out=x_dst[:, 2:8, :], in_=x_src[:, 2:8, :])
-            load_mask(2, 0, N)
+            for k in range(4):
+                load_mask(2, 512 * k, 512 * k + 512)
             make_identity(nc, ident_bf[:])
             make_identity(nc, ident_f[:])
 
@@ -259,10 +260,10 @@ def tile_attention_kernel(tc, x, W, b, neighbor_mask, out):
                     load_mask(u + 3, 0, N)
                 if u - 1 >= 0:
                     exp_sum(u - 1)
-                if u - 3 >= 0:
-                    transpose_att(u - 3)
                 if 1 <= u and u + 1 < T:
                     scores(u + 1, 3)
+                if u - 3 >= 0:
+                    transpose_att(u - 3)
                 for k in range(3):
                     if u == 0:
                         conv(0, 512 * k, 512 * k + 512, "vector")
@@ -275,7 +276,10 @@ def tile_attention_kernel(tc, x, W, b, neighbor_mask, out):
                     scores(1, 3)
                     for q in range(1, 4):
                         flip(xT, x_sb, q, "scalar")
-                if 1 <= u and u + 1 < T:
+                if u == 1:
+                    for k in range(4):
+                        conv(2, 512 * k, 512 * k + 512, "scalar")
+                if 2 <= u and u + 1 < T:
                     conv(u + 1, 0, N, "scalar")
                 if u + 1 < T:
                     fetch_last_bank(u + 1)

@@ -91,15 +91,17 @@ def tile_attention_kernel(tc, x, W, b, neighbor_mask, out):
                 z = ps_z.tile([P, 512], F32, tag="z", name="z")
             else:
                 z = ps_z3.tile([P, 512], F32, tag="z3", name="z3")
+            nc.tensor.matmul(
+                out=z[:], lhsT=xT[:, t, :],
+                rhs=wT[:, 4 * k : 4 * k + 4, :].rearrange("d k c -> d (k c)"),
+                start=True, stop=False,
+            )
             for q in range(4):
                 kb = 4 * k + q
-                cols = slice(128 * q, 128 * q + 128)
                 nc.tensor.matmul(
-                    out=z[:, cols], lhsT=xT[:, t, :], rhs=wT[:, kb, :], start=True, stop=False
-                )
-                nc.tensor.matmul(
-                    out=z[:, cols], lhsT=bcol[:, kb : kb + 1].to_broadcast([P, P]),
-                    rhs=ident_f[:], is_transpose=True, start=False, stop=True,
+                    out=z[:, 128 * q : 128 * q + 128],
+                    lhsT=bcol[:, kb : kb + 1].to_broadcast([P, P]),
+                    rhs=ident_f[:], is_transpose=True, start=False, stop=(q == 3),
                 )
             st[("z", t, k)] = z
 

@@ -170,24 +170,25 @@ def tile_attention_kernel(tc, x, W, b, neighbor_mask, out):
                 )
             st[("att", t)] = att
 
-        def transpose_att(t, engines=("scalar", "scalar")):
+        def flip_att(t):
             att_words = st[("att", t)][:].bitcast(F32)
-            grouped = work.tile([P, N], BF16, tag="grouped", name="grouped", align_bytes=64, bufs=4)
-            grouped_words = grouped[:].bitcast(F32).rearrange("p (c i u) -> p c i u", c=G, i=P, u=2)
             for half in range(2):
                 tp = ps_t.tile([P, 4, P], F32, tag="t", name="tp")
                 for k in range(4):
                     first = 128 * (4 * half + k)
                     nc.tensor.transpose(tp[:, k, :], att_words[:, first : first + 128], ident_f[:])
-                if engines[half] == "scalar":
-                    nc.scalar.copy(
-                        out=grouped_words[:, 2 * half : 2 * half + 2, :, :],
-                        in_=tp[:].rearrange("p (c u) i -> p c i u", u=2),
-                    )
+                st[("tp", t, half)] = tp
+
+        def regroup(t, engine):
+            grouped = work.tile([P, N], BF16, tag="grouped", name="grouped", align_bytes=64, bufs=4)
+            grouped_words = grouped[:].bitcast(F32).rearrange("p (c i u) -> p c i u", c=G, i=P, u=2)
+            for half in range(2):
+                src = st[("tp", t, half)][:].rearrange("p (c u) i -> p c i u", u=2)
+                if engine == "scalar":
+                    nc.scalar.copy(out=grouped_words[:, 2 * half : 2 * half + 2, :, :], in_=src)
                 else:
                     nc.vector.tensor_copy(
-                        out=grouped_words[:, 2 * half : 2 * half + 2, :, :],
-                        in_=tp[:].rearrange("p (c u) i -> p c i u", u=2),
+                        out=grouped_words[:, 2 * half : 2 * half + 2, :, :], in_=src
                     )
             st[("grouped", t)] = grouped
 
@@ -260,12 +261,16 @@ def tile_attention_kernel(tc, x, W, b, neighbor_mask, out):
             for u in range(T):
                 if u + 3 < T:
                     load_mask(u + 3, 0, N)
+                if u - 5 >= 0:
+                    multiply(u - 5)
                 if u - 1 >= 0:
                     exp_sum(u - 1)
+                if u - 5 >= 0:
+                    store(u - 5)
                 if 1 <= u and u + 1 < T:
                     scores(u + 1, 3)
                 if u - 3 >= 0:
-                    transpose_att(u - 3)
+                    flip_att(u - 3)
                 for k in range(3):
                     if u == 0:
                         conv(0, 512 * k, 512 * k + 512, "vector")
@@ -283,6 +288,8 @@ def tile_attention_kernel(tc, x, W, b, neighbor_mask, out):
                         conv(2, 512 * k, 512 * k + 512, "scalar")
                 if 2 <= u and u + 1 < T:
                     conv(u + 1, 0, N, "scalar")
+                if u - 3 >= 0:
+                    regroup(u - 3, "scalar")
                 if u + 1 < T:
                     fetch_last_bank(u + 1)
                 if u == 0:
@@ -294,8 +301,6 @@ def tile_attention_kernel(tc, x, W, b, neighbor_mask, out):
                 leaky(u)
                 if u - 4 >= 0:
                     quantise(u - 4)
-                    multiply(u - 4)
-                    store(u - 4)
                 if u == 1:
                     nc.vector.quantize_mx(
                         out=xq[:].bitcast(FP8X4), scales=xs[:],
@@ -307,12 +312,17 @@ def tile_attention_kernel(tc, x, W, b, neighbor_mask, out):
                     add_mask_last_bank(u + 1)
                 row_max(u)
 
+            multiply(T - 5)
             exp_sum(T - 1)
+            store(T - 5)
             normalise(T - 2, "vector")
-            transpose_att(T - 3, ("vector", "vector"))
-            transpose_att(T - 2)
+            flip_att(T - 3)
+            regroup(T - 3, "vector")
+            flip_att(T - 2)
+            regroup(T - 2, "scalar")
             normalise(T - 1, "vector")
-            transpose_att(T - 1)
+            flip_att(T - 1)
+            regroup(T - 1, "scalar")
             for t in range(T - 4, T):
                 quantise(t)
                 multiply(t)

@@ -20,6 +20,7 @@ G = 4
 T = N // P
 FLOPS = 2 * 2 * N * N * D
 BIG = 2.0**125
+REST = 384
 
 
 def tile_attention_kernel(tc, x, W, b, neighbor_mask, out):
@@ -155,20 +156,27 @@ def tile_attention_kernel(tc, x, W, b, neighbor_mask, out):
             st[("e", t)] = e
             st[("ssum", t)] = ssum
 
-        def normalise(t, engine):
+        def normalise(t, engine, rest=0):
             rinv = small.tile([P, 1], F32, tag="rinv", name="rinv")
             nc.vector.reciprocal(out=rinv[:], in_=st[("ssum", t)][:])
             att = work.tile([P, N], BF16, tag="att", name="att")
+            st[("rinv", t)] = rinv
             if engine == "gpsimd":
                 nc.gpsimd.tensor_scalar(
-                    out=att[:], in0=st[("e", t)][:], scalar1=rinv[:], scalar2=0.0,
-                    op0=ALU.mult, op1=ALU.add,
+                    out=att[:, 0 : N - rest], in0=st[("e", t)][:, 0 : N - rest], scalar1=rinv[:],
+                    scalar2=0.0, op0=ALU.mult, op1=ALU.add,
                 )
             else:
                 nc.vector.tensor_scalar(
                     out=att[:], in0=st[("e", t)][:], scalar1=rinv[:], scalar2=None, op0=ALU.mult
                 )
             st[("att", t)] = att
+
+        def normalise_rest(t):
+            nc.scalar.activation(
+                out=st[("att", t)][:, N - REST : N], in_=st[("e", t)][:, N - REST : N],
+                func=ACT.Copy, scale=st[("rinv", t)][:],
+            )
 
         def flip_att(t):
             att_words = st[("att", t)][:].bitcast(F32)
@@ -267,16 +275,18 @@ def tile_attention_kernel(tc, x, W, b, neighbor_mask, out):
                     exp_sum(u - 1)
                 if u - 5 >= 0:
                     store(u - 5)
+                if u - 3 >= 0:
+                    normalise_rest(u - 3)
                 if 1 <= u and u + 1 < T:
                     scores(u + 1, 3)
-                if u - 3 >= 0:
-                    flip_att(u - 3)
                 for k in range(3):
                     if u == 0:
                         conv(0, 512 * k, 512 * k + 512, "vector")
                     add_mask(u, k)
                     if u + 1 < T:
                         scores(u + 1, k)
+                if u - 3 >= 0:
+                    flip_att(u - 3)
                 if u == 0:
                     conv(0, 1536, 2048, "vector")
                     add_mask(0, 3)
@@ -288,10 +298,10 @@ def tile_attention_kernel(tc, x, W, b, neighbor_mask, out):
                         conv(2, 512 * k, 512 * k + 512, "scalar")
                 if 2 <= u and u + 1 < T:
                     conv(u + 1, 0, N, "scalar")
-                if u - 3 >= 0:
-                    regroup(u - 3, "scalar")
                 if u + 1 < T:
                     fetch_last_bank(u + 1)
+                if u - 3 >= 0:
+                    regroup(u - 3, "scalar")
                 if u == 0:
                     for g in range(G):
                         nc.scalar.copy(
@@ -307,7 +317,10 @@ def tile_attention_kernel(tc, x, W, b, neighbor_mask, out):
                         in_=gx[:].rearrange("p g d t -> p (g d t)"),
                     )
                 if u - 2 >= 0:
-                    normalise(u - 2, "gpsimd")
+                    if u + 1 < T:
+                        normalise(u - 2, "gpsimd", REST)
+                    else:
+                        normalise(u - 2, "gpsimd")
                 if u + 1 < T:
                     add_mask_last_bank(u + 1)
                 row_max(u)

from contextlib import ExitStack

import concourse.mybir as mybir
from concourse.masks import make_identity

F32 = mybir.dt.float32
BF16 = mybir.dt.bfloat16
I32 = mybir.dt.int32
U32 = mybir.dt.uint32
U8 = mybir.dt.uint8
FP8X4 = mybir.dt.float8_e4m3fn_x4
ALU = mybir.AluOpType
ACT = mybir.ActivationFunctionType
AX = mybir.AxisListType

P = 128
N = 2048
D = 128
G = 4
T = N // P
FLOPS = 2 * 2 * N * N * D
BIG = 2.0**125
REST = 384


def tile_attention_kernel(tc, x, W, b, neighbor_mask, out):
    nc = tc.nc
    with ExitStack() as ctx:
        keep = ctx.enter_context(tc.tile_pool(name="keep", bufs=1))
        work = ctx.enter_context(tc.tile_pool(name="work", bufs=2))
        maskp = ctx.enter_context(tc.tile_pool(name="maskp", bufs=3))
        small = ctx.enter_context(tc.tile_pool(name="small", bufs=4))
        ps_z = ctx.enter_context(tc.psum_pool(name="ps_z", bufs=3))
        ps_z3 = ctx.enter_context(tc.psum_pool(name="ps_z3", bufs=1))
        ps_t = ctx.enter_context(tc.psum_pool(name="ps_t", bufs=2))
        ps_o = ctx.enter_context(tc.psum_pool(name="ps_o", bufs=2))

        mask_words = neighbor_mask.bitcast(I32).rearrange("(q p e) w -> p q e w", q=8, p=P, e=2)
        out_rows = out[0].rearrange("(q p e) d -> p q (e d)", q=8, p=P, e=2)
        w_rows = W[0].rearrange("(k p) d -> p k d", p=P)
        st = {}

        xT = keep.tile([P, T, P], BF16)
        wT = keep.tile([P, T, P], BF16)
        bcol = keep.tile([P, T], F32)
        gx = keep.tile([P, G, D, 4], BF16, align_bytes=64)
        xq = keep.tile([P, G * D], U32, align_bytes=64)
        xs = keep.tile([P, G * D], U8, align_bytes=64)
        b16 = keep.tile([P, P], BF16)
        x_sb = keep.tile([P, T, D], BF16)
        w_sb = keep.tile([P, T, D], BF16)
        ident_bf = keep.tile([P, P], BF16)
        ident_f = keep.tile([P, P], F32)

        def load_mask(t, first, last):
            if first == 0:
                st[("m", t)] = maskp.tile([P, 2 * N], I32, tag="m_t", name="m_t")
            nc.sync.dma_start(
                out=st[("m", t)][:, 2 * first : 2 * last],
                in_=mask_words[:, t // 2, t % 2, 2 * first : 2 * last],
            )

        def flip(dst, src, q, engine):
            tp = ps_t.tile([P, 4, P], BF16, tag="t", name="tpb")
            for k in range(4):
                nc.tensor.transpose(tp[:, k, :], src[:, 4 * q + k, :], ident_bf[:])
            if engine == "vector":
                nc.vector.tensor_copy(out=dst[:, 4 * q : 4 * q + 4, :], in_=tp[:])
            else:
                nc.scalar.copy(out=dst[:, 4 * q : 4 * q + 4, :], in_=tp[:])

        def conv(t, first, last, engine):
            if first == 0:
                st[("pm", t)] = work.tile([P, N], BF16, tag="pm", name="pm", bufs=3)
            pm = st[("pm", t)]
            m_t = st[("m", t)]
            if engine == "vector":
                nc.vector.tensor_scalar(
                    out=pm[:, first:last],
                    in0=m_t[:].rearrange("p (j two) -> p j two", two=2)[:, first:last, 0],
                    scalar1=-1.0, scalar2=BIG, op0=ALU.add, op1=ALU.mult,
                )
            else:
                nc.scalar.activation(
                    out=pm[:, first:last],
                    in_=m_t[:].bitcast(U32).rearrange("p (j two) -> p j two", two=2)[:, first:last, 0],
                    func=ACT.Copy, scale=BIG, bias=-BIG,
                )

        def scores(t, k):
            if k < 3:
                z = ps_z.tile([P, 512], F32, tag="z", name="z")
            else:
                z = ps_z3.tile([P, 512], F32, tag="z3", name="z3")
            nc.tensor.matmul(
                out=z[:], lhsT=xT[:, t, :],
                rhs=wT[:, 4 * k : 4 * k + 4, :].rearrange("d k c -> d (k c)"),
                start=True, stop=False,
            )
            for q in range(4):
                kb = 4 * k + q
                nc.tensor.matmul(
                    out=z[:, 128 * q : 128 * q + 128],
                    lhsT=bcol[:, kb : kb + 1].to_broadcast([P, P]),
                    rhs=ident_f[:], is_transpose=True, start=False, stop=(q == 3),
                )
            st[("z", t, k)] = z

        def new_vm(t):
            st[("vm", t)] = work.tile([P, N], F32, tag="vm", name="vm")

        def fetch_last_bank(t):
            zb = work.tile([P, 512], F32, tag="zb", name="zb")
            nc.scalar.copy(out=zb[:], in_=st[("z", t, 3)][:])
            st[("zb", t)] = zb

        def add_mask_last_bank(t):
            new_vm(t)
            nc.gpsimd.tensor_tensor(
                out=st[("vm", t)][:, 1536:2048], in0=st[("zb", t)][:],
                in1=st[("pm", t)][:, 1536:2048], op=ALU.add,
            )

        def add_mask(t, k):
            cols = slice(512 * k, 512 * k + 512)
            nc.vector.tensor_tensor(
                out=st[("vm", t)][:, cols], in0=st[("z", t, k)][:], in1=st[("pm", t)][:, cols],
                op=ALU.add,
            )

        def leaky(t):
            vm = st[("vm", t)]
            s = work.tile([P, N], F32, tag="s", name="s")
            for h in range(2):
                cols = slice(1024 * h, 1024 * h + 1024)
                nc.vector.scalar_tensor_tensor(
                    out=s[:, cols], in0=vm[:, cols], scalar=0.2, in1=vm[:, cols],
                    op0=ALU.mult, op1=ALU.max,
                )
            st[("s", t)] = s

        def row_max(t):
            negm = small.tile([P, 1], F32, tag="negm", name="negm")
            nc.vector.tensor_reduce(
                out=negm[:], in_=st[("s", t)][:], axis=AX.X, op=ALU.max, negate=True
            )
            st[("negm", t)] = negm

        def exp_sum(t):
            e = work.tile([P, N], F32, tag="e", name="e", bufs=3)
            ssum = small.tile([P, 1], F32, tag="ssum", name="ssum")
            nc.scalar.activation(
                out=e[:], in_=st[("s", t)][:], func=ACT.Exp, bias=st[("negm", t)][:], scale=1.0,
                accum_out=ssum[:],
            )
            st[("e", t)] = e
            st[("ssum", t)] = ssum

        def normalise(t, engine, rest=0):
            rinv = small.tile([P, 1], F32, tag="rinv", name="rinv")
            nc.vector.reciprocal(out=rinv[:], in_=st[("ssum", t)][:])
            att = work.tile([P, N], BF16, tag="att", name="att")
            st[("rinv", t)] = rinv
            if engine == "gpsimd":
                nc.gpsimd.tensor_scalar(
                    out=att[:, 0 : N - rest], in0=st[("e", t)][:, 0 : N - rest], scalar1=rinv[:],
                    scalar2=0.0, op0=ALU.mult, op1=ALU.add,
                )
            else:
                nc.vector.tensor_scalar(
                    out=att[:], in0=st[("e", t)][:], scalar1=rinv[:], scalar2=None, op0=ALU.mult
                )
            st[("att", t)] = att

        def normalise_rest(t):
            nc.scalar.activation(
                out=st[("att", t)][:, N - REST : N], in_=st[("e", t)][:, N - REST : N],
                func=ACT.Copy, scale=st[("rinv", t)][:],
            )

        def flip_att(t):
            att_words = st[("att", t)][:].bitcast(F32)
            for half in range(2):
                tp = ps_t.tile([P, 4, P], F32, tag="t", name="tp")
                for k in range(4):
                    first = 128 * (4 * half + k)
                    nc.tensor.transpose(tp[:, k, :], att_words[:, first : first + 128], ident_f[:])
                st[("tp", t, half)] = tp

        def regroup(t, engine):
            grouped = work.tile([P, N], BF16, tag="grouped", name="grouped", align_bytes=64, bufs=4)
            grouped_words = grouped[:].bitcast(F32).rearrange("p (c i u) -> p c i u", c=G, i=P, u=2)
            for half in range(2):
                src = st[("tp", t, half)][:].rearrange("p (c u) i -> p c i u", u=2)
                if engine == "scalar":
                    nc.scalar.copy(out=grouped_words[:, 2 * half : 2 * half + 2, :, :], in_=src)
                else:
                    nc.vector.tensor_copy(
                        out=grouped_words[:, 2 * half : 2 * half + 2, :, :], in_=src
                    )
            st[("grouped", t)] = grouped

        def quantise(t):
            aq = work.tile([P, G * P], U32, tag="aq", name="aq", align_bytes=64)
            asc = work.tile([P, G * P], U8, tag="asc", name="asc", align_bytes=64)
            nc.vector.quantize_mx(
                out=aq[:].bitcast(FP8X4), scales=asc[:], in_=st[("grouped", t)][:]
            )
            st[("aq", t)] = aq
            st[("asc", t)] = asc

        def multiply(t):
            aq = st[("aq", t)]
            asc = st[("asc", t)]
            o_ps = ps_o.tile([P, D], F32, tag="o", name="o_ps")
            for c in range(G):
                cols = slice(128 * c, 128 * c + 128)
                nc.tensor.matmul_mx(
                    out=o_ps[:],
                    lhsT=aq[:, cols].bitcast(FP8X4), lhsT_scale=asc[:, cols],
                    rhs=xq[:, cols].bitcast(FP8X4), rhs_scale=xs[:, cols],
                    start=(c == 0), stop=(c == G - 1),
                )
            st[("o", t)] = o_ps

        def store(t):
            if t % 2 == 0:
                st["o_sb"] = work.tile([P, 2, D], F32, tag="o_sb", name="o_sb")
            o_sb = st["o_sb"]
            nc.scalar.copy(out=o_sb[:, t % 2, :], in_=st[("o", t)][:])
            if t % 2 == 1:
                nc.sync.dma_start(
                    out=out_rows[:, t // 2, :], in_=o_sb[:].rearrange("p e d -> p (e d)")
                )

        with tc.manual_schedule():
            nc.gpsimd.memset(b16[:], 0.0)
            nc.scalar.dma_start(out=b16[0:16, :], in_=b[0].rearrange("(r c) -> r c", c=P))
            x_dst = x_sb[:].rearrange("p (q e) d -> p q (e d)", e=2)
            x_src = x[0].rearrange("(q p e) d -> p q (e d)", q=8, p=P, e=2)
            for k in range(4):
                nc.sync.dma_start(
                    out=w_sb[:, 4 * k : 4 * k + 4, :], in_=w_rows[:, 4 * k : 4 * k + 4, :]
                )
                if k == 0:
                    nc.sync.dma_start(out=x_dst[:, 0:2, :], in_=x_src[:, 0:2, :])
                load_mask(0, 512 * k, 512 * k + 512)
            for k in range(4):
                load_mask(1, 512 * k, 512 * k + 512)
            nc.sync.dma_start(out=x_dst[:, 2:8, :], in_=x_src[:, 2:8, :])
            for k in range(4):
                load_mask(2, 512 * k, 512 * k + 512)
            make_identity(nc, ident_bf[:])
            make_identity(nc, ident_f[:])

            flip(wT, w_sb, 0, "scalar")
            flip(xT, x_sb, 0, "vector")
            tb = ps_t.tile([P, P], BF16, tag="t")
            nc.tensor.transpose(tb[:], b16[:], ident_bf[:])
            nc.vector.tensor_copy(out=bcol[:], in_=tb[:, 0:T])
            scores(0, 0)
            for k in range(1, 4):
                flip(wT, w_sb, k, "scalar")
                scores(0, k)
            for k in range(4):
                conv(1, 512 * k, 512 * k + 512, "scalar")
            new_vm(0)

            for u in range(T):
                if u + 3 < T:
                    load_mask(u + 3, 0, N)
                if u - 5 >= 0:
                    multiply(u - 5)
                if u - 1 >= 0:
                    exp_sum(u - 1)
                if u - 5 >= 0:
                    store(u - 5)
                if u - 3 >= 0:
                    normalise_rest(u - 3)
                if 1 <= u and u + 1 < T:
                    scores(u + 1, 3)
                for k in range(3):
                    if u == 0:
                        conv(0, 512 * k, 512 * k + 512, "vector")
                    add_mask(u, k)
                    if u + 1 < T:
                        scores(u + 1, k)
                if u - 3 >= 0:
                    flip_att(u - 3)
                if u == 0:
                    conv(0, 1536, 2048, "vector")
                    add_mask(0, 3)
                    scores(1, 3)
                    for q in range(1, 4):
                        flip(xT, x_sb, q, "scalar")
                if u == 1:
                    for k in range(4):
                        conv(2, 512 * k, 512 * k + 512, "scalar")
                if 2 <= u and u + 1 < T:
                    conv(u + 1, 0, N, "scalar")
                if u + 1 < T:
                    fetch_last_bank(u + 1)
                if u - 3 >= 0:
                    regroup(u - 3, "scalar")
                if u == 0:
                    for g in range(G):
                        nc.scalar.copy(
                            out=gx[:, g, :, :],
                            in_=x_sb[:, 4 * g : 4 * g + 4, :].rearrange("p t d -> p d t"),
                        )
                leaky(u)
                if u - 4 >= 0:
                    quantise(u - 4)
                if u == 1:
                    nc.vector.quantize_mx(
                        out=xq[:].bitcast(FP8X4), scales=xs[:],
                        in_=gx[:].rearrange("p g d t -> p (g d t)"),
                    )
                if u - 2 >= 0:
                    if u + 1 < T:
                        normalise(u - 2, "gpsimd", REST)
                    else:
                        normalise(u - 2, "gpsimd")
                if u + 1 < T:
                    add_mask_last_bank(u + 1)
                row_max(u)

            multiply(T - 5)
            exp_sum(T - 1)
            store(T - 5)
            normalise(T - 2, "vector")
            flip_att(T - 3)
            regroup(T - 3, "vector")
            flip_att(T - 2)
            regroup(T - 2, "scalar")
            normalise(T - 1, "vector")
            flip_att(T - 1)
            regroup(T - 1, "scalar")
            for t in range(T - 4, T):
                quantise(t)
                multiply(t)
                store(t)
